import numpy as np
import ml_dtypes


def mxq(x, axis, fmt="e4m3"):
    dtype, down = {"e4m3": (ml_dtypes.float8_e4m3fn, 7), "e5m2": (ml_dtypes.float8_e5m2, 14)}[fmt]
    v = np.moveaxis(np.asarray(x, np.float32).astype(ml_dtypes.bfloat16).astype(np.float64), axis, -1)
    blocks = v.reshape(v.shape[:-1] + (-1, 32))
    amax = np.abs(blocks).max(-1, keepdims=True)
    byte = np.maximum(np.where(amax > 0, np.frexp(amax)[1] - 1 + 127, 0) - down, 1)
    scale = np.exp2(byte - 127.0)
    codes = (blocks / scale).astype(np.float32).astype(dtype).astype(np.float64)
    return np.moveaxis((codes * scale).reshape(v.shape), -1, axis)


WIDE = False


def mx_kscale(k):
    if not WIDE:
        return np.ones(k)
    levels = np.array([20, -20, 10, -10, 0])
    a = np.random.permutation(np.resize(levels, k // 512 * 4)).reshape(k // 512, 4)
    idx = np.arange(k)
    return np.exp2(a[idx // 512, idx % 128 // 32])


BF16 = ml_dtypes.bfloat16


def bf(x):
    return np.asarray(x, np.float32).astype(BF16)


def f64(x):
    return np.asarray(x).astype(np.float64)


B, NH, T, D, N = 1, 1, 256, 512, 8192
THETA = 2.0 ** 16
SCALE = N ** -0.5


def rope_tables():
    pair = np.repeat(np.arange(N // 2), 2)
    freqs = 1.0 / THETA ** (pair * 2.0 / N)
    angles = np.arange(T)[:, None] * freqs[None, :]
    return np.cos(angles), np.sin(angles)


def rope(v, cos, sin):
    v_rot = np.stack([-v[..., 1::2], v[..., ::2]], axis=-1).reshape(v.shape)
    return v * cos + v_rot * sin


def rope_adjoint(h, cos, sin):
    hs = h * sin
    hs_rot = np.stack([hs[..., 1::2], -hs[..., ::2]], axis=-1).reshape(h.shape)
    return h * cos + hs_rot


def setup_inputs():
    u = mx_kscale(D)
    cos, sin = rope_tables()
    Q = np.random.uniform(size=(B, NH, T, N)) * 1.2 / N ** 0.25
    V = np.random.standard_normal((B, 1, T, D)) * 45.0 / np.sqrt(T) / u
    state = np.random.standard_normal((B, NH, N, D)) * 60.0 / N ** 0.75 / u
    g = np.random.standard_normal((B, NH, N, D)) * np.exp2(np.random.randint(-12, 1, (B, NH, N, 1))) * 32.0 * u
    return {"Q": bf(Q), "V": bf(V), "state": bf(state), "cos": bf(cos), "sin": bf(sin), "grad_out": bf(g)}


def reference(Q, V, state, cos, sin, grad_out):
    gQR = (mxq(f64(V), 3, "e4m3") @ np.swapaxes(mxq(f64(grad_out), 3, "e5m2"), -2, -1)) * SCALE
    return rope_adjoint(gQR, f64(cos), f64(sin))

@@ -1,0 +1,197 @@
+from contextlib import ExitStack
+
+import concourse.mybir as mybir
+from concourse.masks import make_identity
+
+F32 = mybir.dt.float32
+BF16 = mybir.dt.bfloat16
+U32 = mybir.dt.uint32
+U8 = mybir.dt.uint8
+E4M3_X4 = mybir.dt.float8_e4m3fn_x4
+E5M2_X4 = mybir.dt.float8_e5m2_x4
+MULT = mybir.AluOpType.mult
+ADD = mybir.AluOpType.add
+
+P = 128
+T = 256
+D = 512
+N = 8192
+SCALE = N**-0.5
+
+PACK = 4
+WORDS = D // 2
+T_TILES = T // P
+ROWS = 8
+BLOCK = P * ROWS
+BLOCKS = N // BLOCK
+BANK = 512
+PAIRS = BANK // 2
+BANKS_PER_BLOCK = BLOCK // BANK
+Q_PER_BANK = P // BANKS_PER_BLOCK
+TABLE = 2 * BLOCK
+TABLES = N // TABLE
+AHEAD = 2
+
+FLOPS = 2 * T * N * D
+BYTES = 2 * (T * D + N * D + 2 * T * N) + 4 * T * N
+
+
+def tile_attention_pb_kernel(tc, Q, V, state, cos, sin, grad_out, out):
+    nc = tc.nc
+
+    v_rows = V[0, 0, :, :].rearrange("(tt p) k -> p tt k", p=P)
+    g_rows = grad_out[0, 0, :, :].rearrange("(b q r) k -> b q (r k)", q=P, r=ROWS)
+    cos_rows = cos.rearrange("(tt p) n -> p tt n", p=P)
+    sin_rows = sin.rearrange("(tt p) n -> p tt n", p=P)
+    out_rows = out[0, 0, :, :].rearrange("(tt p) n -> p tt n", p=P)
+
+    with ExitStack() as ctx:
+        const = ctx.enter_context(tc.tile_pool(name="const", bufs=1))
+        g_pool = ctx.enter_context(tc.tile_pool(name="g", bufs=BLOCKS))
+        table_pool = ctx.enter_context(tc.tile_pool(name="table", bufs=TABLES))
+        grouped_pool = ctx.enter_context(tc.tile_pool(name="grouped", bufs=2))
+        code_pool = ctx.enter_context(tc.tile_pool(name="code", bufs=3))
+        result_pool = ctx.enter_context(tc.tile_pool(name="result", bufs=4))
+        crossed_pool = ctx.enter_context(tc.tile_pool(name="crossed", bufs=2))
+        flipped_pool = ctx.enter_context(tc.psum_pool(name="flipped", bufs=4))
+        h_pool = ctx.enter_context(tc.psum_pool(name="h", bufs=4))
+
+        v_sb = const.tile([P, T_TILES * D], BF16)
+        nc.sync.dma_start(out=v_sb[:].rearrange("p (tt k) -> p tt k", tt=T_TILES), in_=v_rows)
+        g_tiles = []
+        cos_tiles = []
+        sin_tiles = []
+        for b in range(BLOCKS):
+            g_sb = g_pool.tile([P, ROWS * D], BF16)
+            nc.sync.dma_start(out=g_sb[:], in_=g_rows[b])
+            g_tiles.append(g_sb)
+            if b % (TABLE // BLOCK) == 0:
+                features = slice(b * BLOCK, b * BLOCK + TABLE)
+                cos_sb = table_pool.tile([P, T_TILES, TABLE], BF16)
+                nc.sync.dma_start(out=cos_sb[:], in_=cos_rows[:, :, features])
+                cos_tiles.append(cos_sb)
+                sin_sb = table_pool.tile([P, T_TILES, TABLE], BF16)
+                nc.sync.dma_start(out=sin_sb[:], in_=sin_rows[:, :, features])
+                sin_tiles.append(sin_sb)
+
+        identity = const.tile([P, P], F32)
+        make_identity(nc, identity[:])
+
+        v_words = v_sb[:].bitcast(F32)
+        v_flipped = flipped_pool.tile([P, BANK], F32, tag="flipped")
+        for u in range(2):
+            for tt in range(T_TILES):
+                nc.tensor.transpose(
+                    v_flipped[:, (u * T_TILES + tt) * P : (u * T_TILES + tt + 1) * P],
+                    v_words[:, tt * WORDS + u * P : tt * WORDS + (u + 1) * P],
+                    identity[:],
+                )
+        v_grouped = const.tile([P, T * PACK], BF16, align_bytes=64)
+        nc.vector.tensor_copy(
+            out=v_grouped[:].bitcast(F32).rearrange("p (t u) -> p t u", u=2),
+            in_=v_flipped[:].rearrange("p (u t) -> p t u", u=2),
+        )
+        v_codes = const.tile([P, T], U32, align_bytes=64)
+        v_scales = const.tile([P, T], U8, align_bytes=64)
+        nc.vector.quantize_mx(out=v_codes[:].bitcast(E4M3_X4), scales=v_scales[:], in_=v_grouped[:])
+
+        def quantise_block(b):
+            g_words = g_tiles[b][:].bitcast(F32)
+            grouped = grouped_pool.tile([P, BLOCK * PACK], BF16, align_bytes=64)
+            grouped_words = grouped[:].bitcast(F32).rearrange(
+                "p (c e s j w) -> p c e s j w", c=BANKS_PER_BLOCK, e=2, s=Q_PER_BANK, j=2, w=4
+            )
+            for e in range(2):
+                for j in range(2):
+                    flipped = flipped_pool.tile([P, BANK], F32, tag="flipped")
+                    for l in range(2):
+                        for u in range(2):
+                            r = 2 * (2 * j + l) + e
+                            w = 2 * l + u
+                            nc.tensor.transpose(
+                                flipped[:, w * P : (w + 1) * P],
+                                g_words[:, r * WORDS + u * P : r * WORDS + (u + 1) * P],
+                                identity[:],
+                            )
+                    nc.scalar.copy(
+                        out=grouped_words[:, :, e, :, j, :],
+                        in_=flipped[:].rearrange(
+                            "p (w c s) -> p c s w", w=4, c=BANKS_PER_BLOCK, s=Q_PER_BANK
+                        ),
+                    )
+            codes = code_pool.tile([P, BLOCK], U32, align_bytes=64)
+            scales = code_pool.tile([P, BLOCK], U8, align_bytes=64)
+            for c in range(BANKS_PER_BLOCK):
+                nc.vector.quantize_mx(
+                    out=codes[:, c * BANK : (c + 1) * BANK].bitcast(E5M2_X4),
+                    scales=scales[:, c * BANK : (c + 1) * BANK],
+                    in_=grouped[:, c * BANK * PACK : (c + 1) * BANK * PACK],
+                )
+            return codes, scales
+
+        def multiply_and_unrope(b, codes, scales):
+            cos_sb = cos_tiles[b * BLOCK // TABLE]
+            sin_sb = sin_tiles[b * BLOCK // TABLE]
+            in_table = b * BLOCK % TABLE
+            result = result_pool.tile([P, T_TILES, BLOCK], F32)
+            crossed = crossed_pool.tile([P, T_TILES, BLOCK], F32)
+            for tt in range(T_TILES):
+                for c in range(BANKS_PER_BLOCK):
+                    bank = slice(c * BANK, (c + 1) * BANK)
+                    tokens = slice(tt * P, (tt + 1) * P)
+                    h = h_pool.tile([P, BANK], F32)
+                    nc.tensor.matmul_mx(
+                        out=h[:],
+                        lhsT=v_codes[:, tokens].bitcast(E4M3_X4),
+                        lhsT_scale=v_scales[:, tokens],
+                        rhs=codes[:, bank].bitcast(E5M2_X4),
+                        rhs_scale=scales[:, bank],
+                        start=True,
+                        stop=True,
+                    )
+                    features = slice(in_table + c * BANK, in_table + (c + 1) * BANK)
+                    cos_pairs = cos_sb[:, tt, features].rearrange("p (i e) -> p i e", e=2)
+                    sin_pairs = sin_sb[:, tt, features].rearrange("p (i e) -> p i e", e=2)
+                    nc.vector.scalar_tensor_tensor(
+                        out=result[:, tt, bank].rearrange("p (i e) -> p i e", e=2),
+                        in0=h[:].rearrange("p (e i) -> p i e", e=2),
+                        scalar=SCALE,
+                        in1=cos_pairs,
+                        op0=MULT,
+                        op1=MULT,
+                    )
+                    nc.vector.scalar_tensor_tensor(
+                        out=crossed[:, tt, c * BANK : c * BANK + PAIRS],
+                        in0=h[:, PAIRS:BANK],
+                        scalar=SCALE,
+                        in1=sin_pairs[:, :, 1],
+                        op0=MULT,
+                        op1=MULT,
+                    )
+                    nc.vector.scalar_tensor_tensor(
+                        out=crossed[:, tt, c * BANK + PAIRS : (c + 1) * BANK],
+                        in0=h[:, 0:PAIRS],
+                        scalar=-SCALE,
+                        in1=sin_pairs[:, :, 0],
+                        op0=MULT,
+                        op1=MULT,
+                    )
+                result_pairs = result[:, tt, :].rearrange(
+                    "p (c i e) -> p c i e", c=BANKS_PER_BLOCK, e=2
+                )
+                nc.gpsimd.tensor_tensor(
+                    out=result_pairs,
+                    in0=result_pairs,
+                    in1=crossed[:, tt, :].rearrange("p (c e i) -> p c i e", c=BANKS_PER_BLOCK, e=2),
+                    op=ADD,
+                )
+                nc.sync.dma_start(
+                    out=out_rows[:, tt, b * BLOCK : (b + 1) * BLOCK], in_=result[:, tt, :]
+                )
+
+        quantised = [quantise_block(b) for b in range(AHEAD)]
+        for b in range(BLOCKS):
+            codes, scales = quantised[b]
+            multiply_and_unrope(b, codes, scales)
+            if b + AHEAD < BLOCKS:
+                quantised.append(quantise_block(b + AHEAD))

@@ -21,16 +21,12 @@ SCALE = N**-0.5
 PACK = 4
 WORDS = D // 2
 T_TILES = T // P
-ROWS = 8
-BLOCK = P * ROWS
-BLOCKS = N // BLOCK
 BANK = 512
+BANKS = N // BANK
 PAIRS = BANK // 2
-BANKS_PER_BLOCK = BLOCK // BANK
-Q_PER_BANK = P // BANKS_PER_BLOCK
-TABLE = 2 * BLOCK
-TABLES = N // TABLE
-AHEAD = 2
+ROWS = BANK // P
+TABLE = 4 * BANK
+STORE = 2 * BANK
 
 FLOPS = 2 * T * N * D
 BYTES = 2 * (T * D + N * D + 2 * T * N) + 4 * T * N
@@ -47,35 +43,38 @@ def tile_attention_pb_kernel(tc, Q, V, state, cos, sin, grad_out, out):
 
     with ExitStack() as ctx:
         const = ctx.enter_context(tc.tile_pool(name="const", bufs=1))
-        g_pool = ctx.enter_context(tc.tile_pool(name="g", bufs=BLOCKS))
-        table_pool = ctx.enter_context(tc.tile_pool(name="table", bufs=TABLES))
-        grouped_pool = ctx.enter_context(tc.tile_pool(name="grouped", bufs=2))
-        code_pool = ctx.enter_context(tc.tile_pool(name="code", bufs=3))
+        g_pool = ctx.enter_context(tc.tile_pool(name="g", bufs=BANKS))
+        grouped_pool = ctx.enter_context(tc.tile_pool(name="grouped", bufs=4))
+        code_pool = ctx.enter_context(tc.tile_pool(name="code", bufs=4))
         result_pool = ctx.enter_context(tc.tile_pool(name="result", bufs=4))
-        crossed_pool = ctx.enter_context(tc.tile_pool(name="crossed", bufs=2))
+        crossed_pool = ctx.enter_context(tc.tile_pool(name="crossed", bufs=3))
         flipped_pool = ctx.enter_context(tc.psum_pool(name="flipped", bufs=4))
         h_pool = ctx.enter_context(tc.psum_pool(name="h", bufs=4))
-
-        v_sb = const.tile([P, T_TILES * D], BF16)
-        nc.sync.dma_start(out=v_sb[:].rearrange("p (tt k) -> p tt k", tt=T_TILES), in_=v_rows)
-        g_tiles = []
-        cos_tiles = []
-        sin_tiles = []
-        for b in range(BLOCKS):
-            g_sb = g_pool.tile([P, ROWS * D], BF16)
-            nc.sync.dma_start(out=g_sb[:], in_=g_rows[b])
-            g_tiles.append(g_sb)
-            if b % (TABLE // BLOCK) == 0:
-                features = slice(b * BLOCK, b * BLOCK + TABLE)
-                cos_sb = table_pool.tile([P, T_TILES, TABLE], BF16)
-                nc.sync.dma_start(out=cos_sb[:], in_=cos_rows[:, :, features])
-                cos_tiles.append(cos_sb)
-                sin_sb = table_pool.tile([P, T_TILES, TABLE], BF16)
-                nc.sync.dma_start(out=sin_sb[:], in_=sin_rows[:, :, features])
-                sin_tiles.append(sin_sb)
+        ctx.enter_context(tc.manual_schedule())
 
         identity = const.tile([P, P], F32)
         make_identity(nc, identity[:])
+
+        v_sb = const.tile([P, T_TILES * D], BF16)
+        nc.sync.dma_start(out=v_sb[:].rearrange("p (tt k) -> p tt k", tt=T_TILES), in_=v_rows)
+        cos_sb = const.tile([P, T_TILES, N], BF16)
+        sin_sb = const.tile([P, T_TILES, N], BF16)
+
+        def load_tables(first, width):
+            features = slice(first, first + width)
+            nc.sync.dma_start(out=cos_sb[:, :, features], in_=cos_rows[:, :, features])
+            nc.sync.dma_start(out=sin_sb[:, :, features], in_=sin_rows[:, :, features])
+
+        g_tiles = []
+        for b in range(BANKS):
+            first = (b - 2) * BANK
+            if first == 0 or first == TABLE // 2:
+                load_tables(first, TABLE // 2)
+            elif first > 0 and first % TABLE == 0:
+                load_tables(first, TABLE)
+            g_sb = g_pool.tile([P, ROWS * D], BF16)
+            nc.sync.dma_start(out=g_sb[:], in_=g_rows[b])
+            g_tiles.append(g_sb)
 
         v_words = v_sb[:].bitcast(F32)
         v_flipped = flipped_pool.tile([P, BANK], F32, tag="flipped")
@@ -95,103 +94,106 @@ def tile_attention_pb_kernel(tc, Q, V, state, cos, sin, grad_out, out):
         v_scales = const.tile([P, T], U8, align_bytes=64)
         nc.vector.quantize_mx(out=v_codes[:].bitcast(E4M3_X4), scales=v_scales[:], in_=v_grouped[:])
 
-        def quantise_block(b):
+        def flip(b):
             g_words = g_tiles[b][:].bitcast(F32)
-            grouped = grouped_pool.tile([P, BLOCK * PACK], BF16, align_bytes=64)
-            grouped_words = grouped[:].bitcast(F32).rearrange(
-                "p (c e s j w) -> p c e s j w", c=BANKS_PER_BLOCK, e=2, s=Q_PER_BANK, j=2, w=4
-            )
+            grouped = grouped_pool.tile([P, BANK * PACK], BF16, align_bytes=64)
+            grouped_words = grouped[:].bitcast(F32)
             for e in range(2):
-                for j in range(2):
-                    flipped = flipped_pool.tile([P, BANK], F32, tag="flipped")
-                    for l in range(2):
-                        for u in range(2):
-                            r = 2 * (2 * j + l) + e
-                            w = 2 * l + u
-                            nc.tensor.transpose(
-                                flipped[:, w * P : (w + 1) * P],
-                                g_words[:, r * WORDS + u * P : r * WORDS + (u + 1) * P],
-                                identity[:],
-                            )
-                    nc.scalar.copy(
-                        out=grouped_words[:, :, e, :, j, :],
-                        in_=flipped[:].rearrange(
-                            "p (w c s) -> p c s w", w=4, c=BANKS_PER_BLOCK, s=Q_PER_BANK
-                        ),
-                    )
-            codes = code_pool.tile([P, BLOCK], U32, align_bytes=64)
-            scales = code_pool.tile([P, BLOCK], U8, align_bytes=64)
-            for c in range(BANKS_PER_BLOCK):
-                nc.vector.quantize_mx(
-                    out=codes[:, c * BANK : (c + 1) * BANK].bitcast(E5M2_X4),
-                    scales=scales[:, c * BANK : (c + 1) * BANK],
-                    in_=grouped[:, c * BANK * PACK : (c + 1) * BANK * PACK],
+                flipped = flipped_pool.tile([P, BANK], F32, tag="flipped")
+                for m in range(2):
+                    for u in range(2):
+                        r = 2 * m + e
+                        w = 2 * m + u
+                        nc.tensor.transpose(
+                            flipped[:, w * P : (w + 1) * P],
+                            g_words[:, r * WORDS + u * P : r * WORDS + (u + 1) * P],
+                            identity[:],
+                        )
+                nc.scalar.copy(
+                    out=grouped_words[:, e * BANK : (e + 1) * BANK].rearrange(
+                        "p (q w) -> p q w", w=4
+                    ),
+                    in_=flipped[:].rearrange("p (w q) -> p q w", w=4),
                 )
+            return grouped
+
+        def quantise(grouped):
+            codes = code_pool.tile([P, BANK], U32, align_bytes=64)
+            scales = code_pool.tile([P, BANK], U8, align_bytes=64)
+            nc.vector.quantize_mx(out=codes[:].bitcast(E5M2_X4), scales=scales[:], in_=grouped[:])
             return codes, scales
 
-        def multiply_and_unrope(b, codes, scales):
-            cos_sb = cos_tiles[b * BLOCK // TABLE]
-            sin_sb = sin_tiles[b * BLOCK // TABLE]
-            in_table = b * BLOCK % TABLE
-            result = result_pool.tile([P, T_TILES, BLOCK], F32)
-            crossed = crossed_pool.tile([P, T_TILES, BLOCK], F32)
+        def multiply(codes, scales):
+            products = []
             for tt in range(T_TILES):
-                for c in range(BANKS_PER_BLOCK):
-                    bank = slice(c * BANK, (c + 1) * BANK)
-                    tokens = slice(tt * P, (tt + 1) * P)
-                    h = h_pool.tile([P, BANK], F32)
-                    nc.tensor.matmul_mx(
-                        out=h[:],
-                        lhsT=v_codes[:, tokens].bitcast(E4M3_X4),
-                        lhsT_scale=v_scales[:, tokens],
-                        rhs=codes[:, bank].bitcast(E5M2_X4),
-                        rhs_scale=scales[:, bank],
-                        start=True,
-                        stop=True,
-                    )
-                    features = slice(in_table + c * BANK, in_table + (c + 1) * BANK)
-                    cos_pairs = cos_sb[:, tt, features].rearrange("p (i e) -> p i e", e=2)
-                    sin_pairs = sin_sb[:, tt, features].rearrange("p (i e) -> p i e", e=2)
-                    nc.vector.scalar_tensor_tensor(
-                        out=result[:, tt, bank].rearrange("p (i e) -> p i e", e=2),
-                        in0=h[:].rearrange("p (e i) -> p i e", e=2),
-                        scalar=SCALE,
-                        in1=cos_pairs,
-                        op0=MULT,
-                        op1=MULT,
-                    )
-                    nc.vector.scalar_tensor_tensor(
-                        out=crossed[:, tt, c * BANK : c * BANK + PAIRS],
-                        in0=h[:, PAIRS:BANK],
-                        scalar=SCALE,
-                        in1=sin_pairs[:, :, 1],
-                        op0=MULT,
-                        op1=MULT,
-                    )
-                    nc.vector.scalar_tensor_tensor(
-                        out=crossed[:, tt, c * BANK + PAIRS : (c + 1) * BANK],
-                        in0=h[:, 0:PAIRS],
-                        scalar=-SCALE,
-                        in1=sin_pairs[:, :, 0],
-                        op0=MULT,
-                        op1=MULT,
-                    )
-                result_pairs = result[:, tt, :].rearrange(
-                    "p (c i e) -> p c i e", c=BANKS_PER_BLOCK, e=2
+                tokens = slice(tt * P, (tt + 1) * P)
+                h = h_pool.tile([P, BANK], F32)
+                nc.tensor.matmul_mx(
+                    out=h[:],
+                    lhsT=v_codes[:, tokens].bitcast(E4M3_X4),
+                    lhsT_scale=v_scales[:, tokens],
+                    rhs=codes[:].bitcast(E5M2_X4),
+                    rhs_scale=scales[:],
+                    start=True,
+                    stop=True,
                 )
-                nc.gpsimd.tensor_tensor(
-                    out=result_pairs,
-                    in0=result_pairs,
-                    in1=crossed[:, tt, :].rearrange("p (c e i) -> p c i e", c=BANKS_PER_BLOCK, e=2),
-                    op=ADD,
-                )
-                nc.sync.dma_start(
-                    out=out_rows[:, tt, b * BLOCK : (b + 1) * BLOCK], in_=result[:, tt, :]
-                )
+                products.append(h)
+            return products
 
-        quantised = [quantise_block(b) for b in range(AHEAD)]
-        for b in range(BLOCKS):
-            codes, scales = quantised[b]
-            multiply_and_unrope(b, codes, scales)
-            if b + AHEAD < BLOCKS:
-                quantised.append(quantise_block(b + AHEAD))
+        def unrope(b, products, result):
+            features = slice(b * BANK, (b + 1) * BANK)
+            columns = slice(b * BANK % STORE, b * BANK % STORE + BANK)
+            crossed = crossed_pool.tile([P, T_TILES, BANK], F32)
+            for tt in range(T_TILES):
+                h = products[tt]
+                sin_pairs = sin_sb[:, tt, features].rearrange("p (i e) -> p i e", e=2)
+                nc.vector.scalar_tensor_tensor(
+                    out=result[:, tt, columns].rearrange("p (i e) -> p i e", e=2),
+                    in0=h[:].rearrange("p (e i) -> p i e", e=2),
+                    scalar=SCALE,
+                    in1=cos_sb[:, tt, features].rearrange("p (i e) -> p i e", e=2),
+                    op0=MULT,
+                    op1=MULT,
+                )
+                nc.vector.scalar_tensor_tensor(
+                    out=crossed[:, tt, 0:PAIRS],
+                    in0=h[:, PAIRS:BANK],
+                    scalar=SCALE,
+                    in1=sin_pairs[:, :, 1],
+                    op0=MULT,
+                    op1=MULT,
+                )
+                nc.vector.scalar_tensor_tensor(
+                    out=crossed[:, tt, PAIRS:BANK],
+                    in0=h[:, 0:PAIRS],
+                    scalar=-SCALE,
+                    in1=sin_pairs[:, :, 0],
+                    op0=MULT,
+                    op1=MULT,
+                )
+            result_pairs = result[:, :, columns].rearrange("p tt (i e) -> p tt i e", e=2)
+            nc.gpsimd.tensor_tensor(
+                out=result_pairs,
+                in0=result_pairs,
+                in1=crossed[:].rearrange("p tt (e i) -> p tt i e", e=2),
+                op=ADD,
+            )
+
+        grouped_next = flip(0)
+        codes, scales = quantise(grouped_next)
+        grouped_next = flip(1)
+        products_next = multiply(codes, scales)
+        for b in range(BANKS):
+            products = products_next
+            if b + 1 < BANKS:
+                grouped = grouped_next
+                if b + 2 < BANKS:
+                    grouped_next = flip(b + 2)
+                codes, scales = quantise(grouped)
+                products_next = multiply(codes, scales)
+            if b * BANK % STORE == 0:
+                result = result_pool.tile([P, T_TILES, STORE], F32)
+            unrope(b, products, result)
+            if (b + 1) * BANK % STORE == 0:
+                stored = slice((b + 1) * BANK - STORE, (b + 1) * BANK)
+                nc.sync.dma_start(out=out_rows[:, :, stored], in_=result[:])

@@ -25,8 +25,13 @@ BANK = 512
 BANKS = N // BANK
 PAIRS = BANK // 2
 ROWS = BANK // P
-TABLE = 4 * BANK
-STORE = 2 * BANK
+STEP_BANKS = 2
+STEP = STEP_BANKS * BANK
+STEPS = T_TILES * N // STEP
+TABLE = 2 * STEP
+QUANTISE_AHEAD = 2
+FLIP_AHEAD = 3
+LOAD_AHEAD = 6
 
 FLOPS = 2 * T * N * D
 BYTES = 2 * (T * D + N * D + 2 * T * N) + 4 * T * N
@@ -37,16 +42,17 @@ def tile_attention_pb_kernel(tc, Q, V, state, cos, sin, grad_out, out):
 
     v_rows = V[0, 0, :, :].rearrange("(tt p) k -> p tt k", p=P)
     g_rows = grad_out[0, 0, :, :].rearrange("(b q r) k -> b q (r k)", q=P, r=ROWS)
-    cos_rows = cos.rearrange("(tt p) n -> p tt n", p=P)
-    sin_rows = sin.rearrange("(tt p) n -> p tt n", p=P)
-    out_rows = out[0, 0, :, :].rearrange("(tt p) n -> p tt n", p=P)
+    cos_rows = cos.rearrange("(tt p) n -> tt p n", p=P)
+    sin_rows = sin.rearrange("(tt p) n -> tt p n", p=P)
+    out_rows = out[0, 0, :, :].rearrange("(tt p) n -> tt p n", p=P)
 
     with ExitStack() as ctx:
         const = ctx.enter_context(tc.tile_pool(name="const", bufs=1))
         g_pool = ctx.enter_context(tc.tile_pool(name="g", bufs=BANKS))
-        grouped_pool = ctx.enter_context(tc.tile_pool(name="grouped", bufs=4))
-        code_pool = ctx.enter_context(tc.tile_pool(name="code", bufs=4))
-        result_pool = ctx.enter_context(tc.tile_pool(name="result", bufs=4))
+        table_pool = ctx.enter_context(tc.tile_pool(name="table", bufs=T_TILES * N // TABLE))
+        grouped_pool = ctx.enter_context(tc.tile_pool(name="grouped", bufs=3))
+        code_pool = ctx.enter_context(tc.tile_pool(name="code", bufs=6))
+        result_pool = ctx.enter_context(tc.tile_pool(name="result", bufs=6))
         crossed_pool = ctx.enter_context(tc.tile_pool(name="crossed", bufs=3))
         flipped_pool = ctx.enter_context(tc.psum_pool(name="flipped", bufs=4))
         h_pool = ctx.enter_context(tc.psum_pool(name="h", bufs=4))
@@ -55,26 +61,34 @@ def tile_attention_pb_kernel(tc, Q, V, state, cos, sin, grad_out, out):
         identity = const.tile([P, P], F32)
         make_identity(nc, identity[:])
 
+
         v_sb = const.tile([P, T_TILES * D], BF16)
         nc.sync.dma_start(out=v_sb[:].rearrange("p (tt k) -> p tt k", tt=T_TILES), in_=v_rows)
-        cos_sb = const.tile([P, T_TILES, N], BF16)
-        sin_sb = const.tile([P, T_TILES, N], BF16)
-
-        def load_tables(first, width):
-            features = slice(first, first + width)
-            nc.sync.dma_start(out=cos_sb[:, :, features], in_=cos_rows[:, :, features])
-            nc.sync.dma_start(out=sin_sb[:, :, features], in_=sin_rows[:, :, features])
-
         g_tiles = []
-        for b in range(BANKS):
-            first = (b - 2) * BANK
-            if first == 0 or first == TABLE // 2:
-                load_tables(first, TABLE // 2)
-            elif first > 0 and first % TABLE == 0:
-                load_tables(first, TABLE)
+
+        def load_bank(b):
             g_sb = g_pool.tile([P, ROWS * D], BF16)
             nc.sync.dma_start(out=g_sb[:], in_=g_rows[b])
             g_tiles.append(g_sb)
+
+        for b in range(FLIP_AHEAD):
+            load_bank(b)
+        tables = {}
+
+        def load_step(s):
+            tt = s % T_TILES
+            first = s // T_TILES * STEP
+            if first % TABLE == 0:
+                cos_sb = table_pool.tile([P, TABLE], BF16)
+                nc.sync.dma_start(out=cos_sb[:], in_=cos_rows[tt, :, first : first + TABLE])
+                sin_sb = table_pool.tile([P, TABLE], BF16)
+                nc.sync.dma_start(out=sin_sb[:], in_=sin_rows[tt, :, first : first + TABLE])
+                tables[(tt, first)] = (cos_sb, sin_sb)
+            if s + FLIP_AHEAD < BANKS:
+                load_bank(s + FLIP_AHEAD)
+
+        for s in range(LOAD_AHEAD):
+            load_step(s)
 
         v_words = v_sb[:].bitcast(F32)
         v_flipped = flipped_pool.tile([P, BANK], F32, tag="flipped")
@@ -93,6 +107,10 @@ def tile_attention_pb_kernel(tc, Q, V, state, cos, sin, grad_out, out):
         v_codes = const.tile([P, T], U32, align_bytes=64)
         v_scales = const.tile([P, T], U8, align_bytes=64)
         nc.vector.quantize_mx(out=v_codes[:].bitcast(E4M3_X4), scales=v_scales[:], in_=v_grouped[:])
+
+        grouped_tiles = {}
+        quantised = {}
+        products = {}
 
         def flip(b):
             g_words = g_tiles[b][:].bitcast(F32)
@@ -115,18 +133,21 @@ def tile_attention_pb_kernel(tc, Q, V, state, cos, sin, grad_out, out):
                     ),
                     in_=flipped[:].rearrange("p (w q) -> p q w", w=4),
                 )
-            return grouped
+            grouped_tiles[b] = grouped
 
-        def quantise(grouped):
+        def quantise(b):
             codes = code_pool.tile([P, BANK], U32, align_bytes=64)
             scales = code_pool.tile([P, BANK], U8, align_bytes=64)
-            nc.vector.quantize_mx(out=codes[:].bitcast(E5M2_X4), scales=scales[:], in_=grouped[:])
-            return codes, scales
+            nc.vector.quantize_mx(
+                out=codes[:].bitcast(E5M2_X4), scales=scales[:], in_=grouped_tiles[b][:]
+            )
+            quantised[b] = (codes, scales)
 
-        def multiply(codes, scales):
-            products = []
-            for tt in range(T_TILES):
-                tokens = slice(tt * P, (tt + 1) * P)
+        def multiply(s):
+            tokens = slice(s % T_TILES * P, (s % T_TILES + 1) * P)
+            products[s] = []
+            for c in range(STEP_BANKS):
+                codes, scales = quantised[s // T_TILES * STEP_BANKS + c]
                 h = h_pool.tile([P, BANK], F32)
                 nc.tensor.matmul_mx(
                     out=h[:],
@@ -137,26 +158,29 @@ def tile_attention_pb_kernel(tc, Q, V, state, cos, sin, grad_out, out):
                     start=True,
                     stop=True,
                 )
-                products.append(h)
-            return products
+                products[s].append(h)
 
-        def unrope(b, products, result):
-            features = slice(b * BANK, (b + 1) * BANK)
-            columns = slice(b * BANK % STORE, b * BANK % STORE + BANK)
-            crossed = crossed_pool.tile([P, T_TILES, BANK], F32)
-            for tt in range(T_TILES):
-                h = products[tt]
-                sin_pairs = sin_sb[:, tt, features].rearrange("p (i e) -> p i e", e=2)
+        def unrope(s):
+            tt = s % T_TILES
+            first = s // T_TILES * STEP
+            cos_sb, sin_sb = tables[(tt, first - first % TABLE)]
+            result = result_pool.tile([P, STEP], F32)
+            crossed = crossed_pool.tile([P, STEP], F32)
+            for c in range(STEP_BANKS):
+                h = products[s][c]
+                bank = slice(c * BANK, (c + 1) * BANK)
+                in_table = slice(first % TABLE + c * BANK, first % TABLE + (c + 1) * BANK)
+                sin_pairs = sin_sb[:, in_table].rearrange("p (i e) -> p i e", e=2)
                 nc.vector.scalar_tensor_tensor(
-                    out=result[:, tt, columns].rearrange("p (i e) -> p i e", e=2),
+                    out=result[:, bank].rearrange("p (i e) -> p i e", e=2),
                     in0=h[:].rearrange("p (e i) -> p i e", e=2),
                     scalar=SCALE,
-                    in1=cos_sb[:, tt, features].rearrange("p (i e) -> p i e", e=2),
+                    in1=cos_sb[:, in_table].rearrange("p (i e) -> p i e", e=2),
                     op0=MULT,
                     op1=MULT,
                 )
                 nc.vector.scalar_tensor_tensor(
-                    out=crossed[:, tt, 0:PAIRS],
+                    out=crossed[:, c * BANK : c * BANK + PAIRS],
                     in0=h[:, PAIRS:BANK],
                     scalar=SCALE,
                     in1=sin_pairs[:, :, 1],
@@ -164,36 +188,34 @@ def tile_attention_pb_kernel(tc, Q, V, state, cos, sin, grad_out, out):
                     op1=MULT,
                 )
                 nc.vector.scalar_tensor_tensor(
-                    out=crossed[:, tt, PAIRS:BANK],
+                    out=crossed[:, c * BANK + PAIRS : (c + 1) * BANK],
                     in0=h[:, 0:PAIRS],
                     scalar=-SCALE,
                     in1=sin_pairs[:, :, 0],
                     op0=MULT,
                     op1=MULT,
                 )
-            result_pairs = result[:, :, columns].rearrange("p tt (i e) -> p tt i e", e=2)
+            result_pairs = result[:].rearrange("p (c i e) -> p c i e", c=STEP_BANKS, e=2)
             nc.gpsimd.tensor_tensor(
                 out=result_pairs,
                 in0=result_pairs,
-                in1=crossed[:].rearrange("p tt (e i) -> p tt i e", e=2),
+                in1=crossed[:].rearrange("p (c e i) -> p c i e", c=STEP_BANKS, e=2),
                 op=ADD,
             )
+            nc.sync.dma_start(out=out_rows[tt, :, first : first + STEP], in_=result[:])
 
-        grouped_next = flip(0)
-        codes, scales = quantise(grouped_next)
-        grouped_next = flip(1)
-        products_next = multiply(codes, scales)
-        for b in range(BANKS):
-            products = products_next
-            if b + 1 < BANKS:
-                grouped = grouped_next
-                if b + 2 < BANKS:
-                    grouped_next = flip(b + 2)
-                codes, scales = quantise(grouped)
-                products_next = multiply(codes, scales)
-            if b * BANK % STORE == 0:
-                result = result_pool.tile([P, T_TILES, STORE], F32)
-            unrope(b, products, result)
-            if (b + 1) * BANK % STORE == 0:
-                stored = slice((b + 1) * BANK - STORE, (b + 1) * BANK)
-                nc.sync.dma_start(out=out_rows[:, :, stored], in_=result[:])
+        for b in range(QUANTISE_AHEAD):
+            flip(b)
+            quantise(b)
+        flip(QUANTISE_AHEAD)
+        multiply(0)
+        for s in range(STEPS):
+            if s + LOAD_AHEAD < STEPS:
+                load_step(s + LOAD_AHEAD)
+            if s + FLIP_AHEAD < BANKS:
+                flip(s + FLIP_AHEAD)
+            if s + QUANTISE_AHEAD < BANKS:
+                quantise(s + QUANTISE_AHEAD)
+            if s + 1 < STEPS:
+                multiply(s + 1)
+            unrope(s)

@@ -31,6 +31,7 @@ STEPS = T_TILES * N // STEP
 TABLE = 2 * STEP
 QUANTISE_AHEAD = 2
 FLIP_AHEAD = 3
+VECTOR_ADDS_EVERY = 8
 LOAD_AHEAD = 6
 
 FLOPS = 2 * T * N * D
@@ -196,7 +197,8 @@ def tile_attention_pb_kernel(tc, Q, V, state, cos, sin, grad_out, out):
                     op1=MULT,
                 )
             result_pairs = result[:].rearrange("p (c i e) -> p c i e", c=STEP_BANKS, e=2)
-            nc.gpsimd.tensor_tensor(
+            adder = nc.vector if s % VECTOR_ADDS_EVERY == VECTOR_ADDS_EVERY - 1 else nc.gpsimd
+            adder.tensor_tensor(
                 out=result_pairs,
                 in0=result_pairs,
                 in1=crossed[:].rearrange("p (c e i) -> p c i e", c=STEP_BANKS, e=2),

@@ -9,6 +9,7 @@ U32 = mybir.dt.uint32
 U8 = mybir.dt.uint8
 E4M3_X4 = mybir.dt.float8_e4m3fn_x4
 E5M2_X4 = mybir.dt.float8_e5m2_x4
+COPY = mybir.ActivationFunctionType.Copy
 MULT = mybir.AluOpType.mult
 ADD = mybir.AluOpType.add
 
@@ -23,7 +24,6 @@ WORDS = D // 2
 T_TILES = T // P
 BANK = 512
 BANKS = N // BANK
-PAIRS = BANK // 2
 ROWS = BANK // P
 STEP_BANKS = 2
 STEP = STEP_BANKS * BANK
@@ -53,8 +53,7 @@ def tile_attention_pb_kernel(tc, Q, V, state, cos, sin, grad_out, out):
         table_pool = ctx.enter_context(tc.tile_pool(name="table", bufs=T_TILES * N // TABLE))
         grouped_pool = ctx.enter_context(tc.tile_pool(name="grouped", bufs=3))
         code_pool = ctx.enter_context(tc.tile_pool(name="code", bufs=6))
-        result_pool = ctx.enter_context(tc.tile_pool(name="result", bufs=6))
-        crossed_pool = ctx.enter_context(tc.tile_pool(name="crossed", bufs=3))
+        term_pool = ctx.enter_context(tc.tile_pool(name="term", bufs=6))
         flipped_pool = ctx.enter_context(tc.psum_pool(name="flipped", bufs=4))
         h_pool = ctx.enter_context(tc.psum_pool(name="h", bufs=4))
         ctx.enter_context(tc.manual_schedule())
@@ -80,11 +79,10 @@ def tile_attention_pb_kernel(tc, Q, V, state, cos, sin, grad_out, out):
             tt = s % T_TILES
             first = s // T_TILES * STEP
             if first % TABLE == 0:
-                cos_sb = table_pool.tile([P, TABLE], BF16)
-                nc.sync.dma_start(out=cos_sb[:], in_=cos_rows[tt, :, first : first + TABLE])
-                sin_sb = table_pool.tile([P, TABLE], BF16)
-                nc.sync.dma_start(out=sin_sb[:], in_=sin_rows[tt, :, first : first + TABLE])
-                tables[(tt, first)] = (cos_sb, sin_sb)
+                table = table_pool.tile([P, 2 * TABLE], BF16)
+                nc.sync.dma_start(out=table[:, 0:TABLE], in_=cos_rows[tt, :, first : first + TABLE])
+                nc.sync.dma_start(out=table[:, TABLE:], in_=sin_rows[tt, :, first : first + TABLE])
+                tables[(tt, first)] = table
             if s + FLIP_AHEAD < BANKS:
                 load_bank(s + FLIP_AHEAD)
 
@@ -116,22 +114,20 @@ def tile_attention_pb_kernel(tc, Q, V, state, cos, sin, grad_out, out):
         def flip(b):
             g_words = g_tiles[b][:].bitcast(F32)
             grouped = grouped_pool.tile([P, BANK * PACK], BF16, align_bytes=64)
-            grouped_words = grouped[:].bitcast(F32)
-            for e in range(2):
+            grouped_words = grouped[:].bitcast(F32).rearrange("p (q m w) -> p m q w", m=2, w=4)
+            for m in range(2):
                 flipped = flipped_pool.tile([P, BANK], F32, tag="flipped")
-                for m in range(2):
+                for e in range(2):
                     for u in range(2):
                         r = 2 * m + e
-                        w = 2 * m + u
+                        w = 2 * e + u
                         nc.tensor.transpose(
                             flipped[:, w * P : (w + 1) * P],
                             g_words[:, r * WORDS + u * P : r * WORDS + (u + 1) * P],
                             identity[:],
                         )
                 nc.scalar.copy(
-                    out=grouped_words[:, e * BANK : (e + 1) * BANK].rearrange(
-                        "p (q w) -> p q w", w=4
-                    ),
+                    out=grouped_words[:, m, :, :],
                     in_=flipped[:].rearrange("p (w q) -> p q w", w=4),
                 )
             grouped_tiles[b] = grouped
@@ -161,54 +157,45 @@ def tile_attention_pb_kernel(tc, Q, V, state, cos, sin, grad_out, out):
                 )
                 products[s].append(h)
 
+        def sign(s):
+            tt = s % T_TILES
+            first = s // T_TILES * STEP
+            in_table = slice(TABLE + first % TABLE, TABLE + first % TABLE + STEP)
+            even = tables[(tt, first - first % TABLE)][:, in_table]
+            even = even.rearrange("p (i e) -> p e i", e=2)[:, 0, :]
+            nc.scalar.activation(out=even, in_=even, func=COPY, scale=-1.0)
+
         def unrope(s):
             tt = s % T_TILES
             first = s // T_TILES * STEP
-            cos_sb, sin_sb = tables[(tt, first - first % TABLE)]
-            result = result_pool.tile([P, STEP], F32)
-            crossed = crossed_pool.tile([P, STEP], F32)
+            table = tables[(tt, first - first % TABLE)][:].rearrange("p (x n) -> p x n", x=2)
+            term = term_pool.tile([P, 2 * STEP], F32)
+            term_planes = term[:].rearrange("p (x n) -> p x n", x=2)
             for c in range(STEP_BANKS):
                 h = products[s][c]
-                bank = slice(c * BANK, (c + 1) * BANK)
                 in_table = slice(first % TABLE + c * BANK, first % TABLE + (c + 1) * BANK)
-                sin_pairs = sin_sb[:, in_table].rearrange("p (i e) -> p i e", e=2)
                 nc.vector.scalar_tensor_tensor(
-                    out=result[:, bank].rearrange("p (i e) -> p i e", e=2),
-                    in0=h[:].rearrange("p (e i) -> p i e", e=2),
+                    out=term_planes[:, :, c * BANK : (c + 1) * BANK],
+                    in0=h[:].unsqueeze(1).to_broadcast([P, 2, BANK]),
                     scalar=SCALE,
-                    in1=cos_sb[:, in_table].rearrange("p (i e) -> p i e", e=2),
+                    in1=table[:, :, in_table],
                     op0=MULT,
                     op1=MULT,
                 )
-                nc.vector.scalar_tensor_tensor(
-                    out=crossed[:, c * BANK : c * BANK + PAIRS],
-                    in0=h[:, PAIRS:BANK],
-                    scalar=SCALE,
-                    in1=sin_pairs[:, :, 1],
-                    op0=MULT,
-                    op1=MULT,
-                )
-                nc.vector.scalar_tensor_tensor(
-                    out=crossed[:, c * BANK + PAIRS : (c + 1) * BANK],
-                    in0=h[:, 0:PAIRS],
-                    scalar=-SCALE,
-                    in1=sin_pairs[:, :, 0],
-                    op0=MULT,
-                    op1=MULT,
-                )
-            result_pairs = result[:].rearrange("p (c i e) -> p c i e", c=STEP_BANKS, e=2)
+            result = term[:, 0:STEP]
             adder = nc.vector if s % VECTOR_ADDS_EVERY == VECTOR_ADDS_EVERY - 1 else nc.gpsimd
             adder.tensor_tensor(
-                out=result_pairs,
-                in0=result_pairs,
-                in1=crossed[:].rearrange("p (c e i) -> p c i e", c=STEP_BANKS, e=2),
+                out=result.rearrange("p (i e) -> p i e", e=2),
+                in0=result.rearrange("p (i e) -> p i e", e=2),
+                in1=term[:, STEP:].rearrange("p (i e) -> p i e", e=2)[:, :, ::-1],
                 op=ADD,
             )
-            nc.sync.dma_start(out=out_rows[tt, :, first : first + STEP], in_=result[:])
+            nc.sync.dma_start(out=out_rows[tt, :, first : first + STEP], in_=result)
 
         for b in range(QUANTISE_AHEAD):
             flip(b)
             quantise(b)
+        sign(0)
         flip(QUANTISE_AHEAD)
         multiply(0)
         for s in range(STEPS):
@@ -216,6 +203,8 @@ def tile_attention_pb_kernel(tc, Q, V, state, cos, sin, grad_out, out):
                 load_step(s + LOAD_AHEAD)
             if s + FLIP_AHEAD < BANKS:
                 flip(s + FLIP_AHEAD)
+            if s + 1 < STEPS:
+                sign(s + 1)
             if s + QUANTISE_AHEAD < BANKS:
                 quantise(s + QUANTISE_AHEAD)
             if s + 1 < STEPS:

@@ -28,11 +28,10 @@ ROWS = BANK // P
 STEP_BANKS = 2
 STEP = STEP_BANKS * BANK
 STEPS = T_TILES * N // STEP
-TABLE = 2 * STEP
+TABLES = {0: STEP, STEP: STEP, 2 * STEP: 2 * STEP, 4 * STEP: 2 * STEP, 6 * STEP: 2 * STEP}
 QUANTISE_AHEAD = 2
 FLIP_AHEAD = 3
-VECTOR_ADDS_EVERY = 8
-LOAD_AHEAD = 6
+LOAD_AHEAD = 7
 
 FLOPS = 2 * T * N * D
 BYTES = 2 * (T * D + N * D + 2 * T * N) + 4 * T * N
@@ -50,10 +49,10 @@ def tile_attention_pb_kernel(tc, Q, V, state, cos, sin, grad_out, out):
     with ExitStack() as ctx:
         const = ctx.enter_context(tc.tile_pool(name="const", bufs=1))
         g_pool = ctx.enter_context(tc.tile_pool(name="g", bufs=BANKS))
-        table_pool = ctx.enter_context(tc.tile_pool(name="table", bufs=T_TILES * N // TABLE))
+        table_pool = ctx.enter_context(tc.tile_pool(name="table", bufs=1))
         grouped_pool = ctx.enter_context(tc.tile_pool(name="grouped", bufs=3))
         code_pool = ctx.enter_context(tc.tile_pool(name="code", bufs=6))
-        term_pool = ctx.enter_context(tc.tile_pool(name="term", bufs=6))
+        term_pool = ctx.enter_context(tc.tile_pool(name="term", bufs=9))
         flipped_pool = ctx.enter_context(tc.psum_pool(name="flipped", bufs=4))
         h_pool = ctx.enter_context(tc.psum_pool(name="h", bufs=4))
         ctx.enter_context(tc.manual_schedule())
@@ -71,20 +70,26 @@ def tile_attention_pb_kernel(tc, Q, V, state, cos, sin, grad_out, out):
             nc.sync.dma_start(out=g_sb[:], in_=g_rows[b])
             g_tiles.append(g_sb)
 
-        for b in range(FLIP_AHEAD):
+        for b in range(QUANTISE_AHEAD):
             load_bank(b)
         tables = {}
 
         def load_step(s):
             tt = s % T_TILES
             first = s // T_TILES * STEP
-            if first % TABLE == 0:
-                table = table_pool.tile([P, 2 * TABLE], BF16)
-                nc.sync.dma_start(out=table[:, 0:TABLE], in_=cos_rows[tt, :, first : first + TABLE])
-                nc.sync.dma_start(out=table[:, TABLE:], in_=sin_rows[tt, :, first : first + TABLE])
-                tables[(tt, first)] = table
-            if s + FLIP_AHEAD < BANKS:
-                load_bank(s + FLIP_AHEAD)
+            if first in TABLES:
+                width = TABLES[first]
+                table = table_pool.tile([P, 2 * width], BF16, name="table_%d" % s)
+                for x, rows in enumerate((cos_rows, sin_rows)):
+                    nc.sync.dma_start(
+                        out=table[:, x * width : (x + 1) * width],
+                        in_=rows[tt, :, first : first + width],
+                    )
+                planes = table[:].rearrange("p (x n) -> p x n", x=2)
+                for c in range(width // STEP):
+                    tables[s + T_TILES * c] = planes[:, :, c * STEP : (c + 1) * STEP]
+            if s + QUANTISE_AHEAD < BANKS:
+                load_bank(s + QUANTISE_AHEAD)
 
         for s in range(LOAD_AHEAD):
             load_step(s)
@@ -109,6 +114,7 @@ def tile_attention_pb_kernel(tc, Q, V, state, cos, sin, grad_out, out):
 
         grouped_tiles = {}
         quantised = {}
+        terms = {}
         products = {}
 
         def flip(b):
@@ -158,55 +164,73 @@ def tile_attention_pb_kernel(tc, Q, V, state, cos, sin, grad_out, out):
                 products[s].append(h)
 
         def sign(s):
-            tt = s % T_TILES
-            first = s // T_TILES * STEP
-            in_table = slice(TABLE + first % TABLE, TABLE + first % TABLE + STEP)
-            even = tables[(tt, first - first % TABLE)][:, in_table]
-            even = even.rearrange("p (i e) -> p e i", e=2)[:, 0, :]
-            nc.scalar.activation(out=even, in_=even, func=COPY, scale=-1.0)
+            even = tables[s][:, 1, :].rearrange("p (i e) -> p e i", e=2)[:, 0, :]
+            if s < T_TILES:
+                nc.gpsimd.tensor_scalar(
+                    out=even, in0=even, scalar1=-1.0, scalar2=0.0, op0=MULT, op1=ADD
+                )
+            else:
+                nc.scalar.activation(out=even, in_=even, func=COPY, scale=-1.0)
 
-        def unrope(s):
-            tt = s % T_TILES
-            first = s // T_TILES * STEP
-            table = tables[(tt, first - first % TABLE)][:].rearrange("p (x n) -> p x n", x=2)
+        def rope_terms(s):
             term = term_pool.tile([P, 2 * STEP], F32)
-            term_planes = term[:].rearrange("p (x n) -> p x n", x=2)
+            terms[s] = term
             for c in range(STEP_BANKS):
-                h = products[s][c]
-                in_table = slice(first % TABLE + c * BANK, first % TABLE + (c + 1) * BANK)
+                bank = slice(c * BANK, (c + 1) * BANK)
                 nc.vector.scalar_tensor_tensor(
-                    out=term_planes[:, :, c * BANK : (c + 1) * BANK],
-                    in0=h[:].unsqueeze(1).to_broadcast([P, 2, BANK]),
+                    out=term[:].rearrange("p (x n) -> p x n", x=2)[:, :, bank],
+                    in0=products[s][c][:].unsqueeze(1).to_broadcast([P, 2, BANK]),
                     scalar=SCALE,
-                    in1=table[:, :, in_table],
+                    in1=tables[s][:, :, bank],
                     op0=MULT,
                     op1=MULT,
                 )
-            result = term[:, 0:STEP]
-            adder = nc.vector if s % VECTOR_ADDS_EVERY == VECTOR_ADDS_EVERY - 1 else nc.gpsimd
-            adder.tensor_tensor(
-                out=result.rearrange("p (i e) -> p i e", e=2),
-                in0=result.rearrange("p (i e) -> p i e", e=2),
-                in1=term[:, STEP:].rearrange("p (i e) -> p i e", e=2)[:, :, ::-1],
-                op=ADD,
-            )
-            nc.sync.dma_start(out=out_rows[tt, :, first : first + STEP], in_=result)
 
-        for b in range(QUANTISE_AHEAD):
+        def add(engine, s, first, width):
+            term = terms[s]
+            pairs = term[:, first : first + width].rearrange("p (i e) -> p i e", e=2)
+            other = term[:, STEP + first : STEP + first + width]
+            other = other.rearrange("p (i e) -> p i e", e=2)[:, :, ::-1]
+            engine.tensor_tensor(out=pairs, in0=pairs, in1=other, op=ADD)
+
+        def store(s, first, width):
+            columns = s // T_TILES * STEP + first
+            nc.sync.dma_start(
+                out=out_rows[s % T_TILES, :, columns : columns + width],
+                in_=terms[s][:, first : first + width],
+            )
+
+        for s in range(T_TILES):
+            sign(s)
+        for b in range(STEP_BANKS):
             flip(b)
             quantise(b)
-        sign(0)
-        flip(QUANTISE_AHEAD)
-        multiply(0)
+        for s in range(T_TILES):
+            multiply(s)
+        flip(STEP_BANKS)
         for s in range(STEPS):
             if s + LOAD_AHEAD < STEPS:
                 load_step(s + LOAD_AHEAD)
             if s + FLIP_AHEAD < BANKS:
                 flip(s + FLIP_AHEAD)
-            if s + 1 < STEPS:
+            if T_TILES <= s + 1 < STEPS:
                 sign(s + 1)
-            if s + QUANTISE_AHEAD < BANKS:
-                quantise(s + QUANTISE_AHEAD)
-            if s + 1 < STEPS:
-                multiply(s + 1)
-            unrope(s)
+            if s < T_TILES:
+                rope_terms(s)
+            if s == T_TILES - 1:
+                for b in range(STEP_BANKS, 2 * STEP_BANKS):
+                    quantise(b)
+                multiply(T_TILES)
+            if s >= T_TILES:
+                if s + QUANTISE_AHEAD < BANKS:
+                    quantise(s + QUANTISE_AHEAD)
+                if s + 1 < STEPS:
+                    multiply(s + 1)
+                rope_terms(s)
+            if s < STEPS - 1:
+                add(nc.gpsimd, s, 0, STEP)
+                store(s, 0, STEP)
+            else:
+                for c in range(STEP_BANKS):
+                    add(nc.vector, s, c * BANK, BANK)
+                    store(s, c * BANK, BANK)

@@ -31,7 +31,7 @@ STEPS = T_TILES * N // STEP
 TABLES = {0: STEP, STEP: STEP, 2 * STEP: 2 * STEP, 4 * STEP: 2 * STEP, 6 * STEP: 2 * STEP}
 QUANTISE_AHEAD = 2
 FLIP_AHEAD = 3
-LOAD_AHEAD = 7
+LOAD_AHEAD = 10
 
 FLOPS = 2 * T * N * D
 BYTES = 2 * (T * D + N * D + 2 * T * N) + 4 * T * N
@@ -52,7 +52,8 @@ def tile_attention_pb_kernel(tc, Q, V, state, cos, sin, grad_out, out):
         table_pool = ctx.enter_context(tc.tile_pool(name="table", bufs=1))
         grouped_pool = ctx.enter_context(tc.tile_pool(name="grouped", bufs=3))
         code_pool = ctx.enter_context(tc.tile_pool(name="code", bufs=6))
-        term_pool = ctx.enter_context(tc.tile_pool(name="term", bufs=9))
+        term_pool = ctx.enter_context(tc.tile_pool(name="term", bufs=3))
+        result_pool = ctx.enter_context(tc.tile_pool(name="result", bufs=12))
         flipped_pool = ctx.enter_context(tc.psum_pool(name="flipped", bufs=4))
         h_pool = ctx.enter_context(tc.psum_pool(name="h", bufs=4))
         ctx.enter_context(tc.manual_schedule())
@@ -115,6 +116,7 @@ def tile_attention_pb_kernel(tc, Q, V, state, cos, sin, grad_out, out):
         grouped_tiles = {}
         quantised = {}
         terms = {}
+        results = {}
         products = {}
 
         def flip(b):
@@ -175,6 +177,8 @@ def tile_attention_pb_kernel(tc, Q, V, state, cos, sin, grad_out, out):
         def rope_terms(s):
             term = term_pool.tile([P, 2 * STEP], F32)
             terms[s] = term
+            result = result_pool.tile([P, STEP], F32)
+            results[s] = result
             for c in range(STEP_BANKS):
                 bank = slice(c * BANK, (c + 1) * BANK)
                 nc.vector.scalar_tensor_tensor(
@@ -187,17 +191,17 @@ def tile_attention_pb_kernel(tc, Q, V, state, cos, sin, grad_out, out):
                 )
 
         def add(engine, s, first, width):
-            term = terms[s]
-            pairs = term[:, first : first + width].rearrange("p (i e) -> p i e", e=2)
-            other = term[:, STEP + first : STEP + first + width]
-            other = other.rearrange("p (i e) -> p i e", e=2)[:, :, ::-1]
-            engine.tensor_tensor(out=pairs, in0=pairs, in1=other, op=ADD)
+            own, other, out = (
+                t[:, c : c + width].rearrange("p (i e) -> p i e", e=2)
+                for t, c in ((terms[s], first), (terms[s], STEP + first), (results[s], first))
+            )
+            engine.tensor_tensor(out=out, in0=own, in1=other[:, :, ::-1], op=ADD)
 
         def store(s, first, width):
             columns = s // T_TILES * STEP + first
             nc.sync.dma_start(
                 out=out_rows[s % T_TILES, :, columns : columns + width],
-                in_=terms[s][:, first : first + width],
+                in_=results[s][:, first : first + width],
             )
 
         for s in range(T_TILES):

@@ -29,8 +29,8 @@ STEP_BANKS = 2
 STEP = STEP_BANKS * BANK
 STEPS = T_TILES * N // STEP
 TABLES = {0: STEP, STEP: STEP, 2 * STEP: 2 * STEP, 4 * STEP: 2 * STEP, 6 * STEP: 2 * STEP}
-QUANTISE_AHEAD = 2
-FLIP_AHEAD = 3
+QUANTISE_AHEAD = 1
+FLIP_AHEAD = 2
 LOAD_AHEAD = 10
 
 FLOPS = 2 * T * N * D
@@ -71,28 +71,40 @@ def tile_attention_pb_kernel(tc, Q, V, state, cos, sin, grad_out, out):
             nc.sync.dma_start(out=g_sb[:], in_=g_rows[b])
             g_tiles.append(g_sb)
 
-        for b in range(QUANTISE_AHEAD):
-            load_bank(b)
         tables = {}
+        table_tiles = {}
 
-        def load_step(s):
+        def load_table(s, x):
             tt = s % T_TILES
             first = s // T_TILES * STEP
             if first in TABLES:
                 width = TABLES[first]
-                table = table_pool.tile([P, 2 * width], BF16, name="table_%d" % s)
-                for x, rows in enumerate((cos_rows, sin_rows)):
-                    nc.sync.dma_start(
-                        out=table[:, x * width : (x + 1) * width],
-                        in_=rows[tt, :, first : first + width],
-                    )
-                planes = table[:].rearrange("p (x n) -> p x n", x=2)
-                for c in range(width // STEP):
-                    tables[s + T_TILES * c] = planes[:, :, c * STEP : (c + 1) * STEP]
-            if s + QUANTISE_AHEAD < BANKS:
-                load_bank(s + QUANTISE_AHEAD)
+                if s not in table_tiles:
+                    table = table_pool.tile([P, 2 * width], BF16, name="table_%d" % s)
+                    table_tiles[s] = table
+                    planes = table[:].rearrange("p (x n) -> p x n", x=2)
+                    for c in range(width // STEP):
+                        tables[s + T_TILES * c] = planes[:, :, c * STEP : (c + 1) * STEP]
+                nc.sync.dma_start(
+                    out=table_tiles[s][:, x * width : (x + 1) * width],
+                    in_=(cos_rows, sin_rows)[x][tt, :, first : first + width],
+                )
 
-        for s in range(LOAD_AHEAD):
+        def load_step(s):
+            load_table(s, 1)
+            load_table(s, 0)
+            if s + FLIP_AHEAD < BANKS:
+                load_bank(s + FLIP_AHEAD)
+
+        load_bank(0)
+        load_table(0, 1)
+        load_bank(1)
+        load_table(0, 0)
+        load_bank(2)
+        load_table(1, 1)
+        load_bank(3)
+        load_table(1, 0)
+        for s in range(T_TILES, LOAD_AHEAD):
             load_step(s)
 
         v_words = v_sb[:].bitcast(F32)
@@ -122,6 +134,7 @@ def tile_attention_pb_kernel(tc, Q, V, state, cos, sin, grad_out, out):
         def flip(b):
             g_words = g_tiles[b][:].bitcast(F32)
             grouped = grouped_pool.tile([P, BANK * PACK], BF16, align_bytes=64)
+            grouped_tiles[b] = grouped
             grouped_words = grouped[:].bitcast(F32).rearrange("p (q m w) -> p m q w", m=2, w=4)
             for m in range(2):
                 flipped = flipped_pool.tile([P, BANK], F32, tag="flipped")
@@ -138,7 +151,6 @@ def tile_attention_pb_kernel(tc, Q, V, state, cos, sin, grad_out, out):
                     out=grouped_words[:, m, :, :],
                     in_=flipped[:].rearrange("p (w q) -> p q w", w=4),
                 )
-            grouped_tiles[b] = grouped
 
         def quantise(b):
             codes = code_pool.tile([P, BANK], U32, align_bytes=64)
@@ -148,22 +160,20 @@ def tile_attention_pb_kernel(tc, Q, V, state, cos, sin, grad_out, out):
             )
             quantised[b] = (codes, scales)
 
-        def multiply(s):
+        def multiply(s, c):
             tokens = slice(s % T_TILES * P, (s % T_TILES + 1) * P)
-            products[s] = []
-            for c in range(STEP_BANKS):
-                codes, scales = quantised[s // T_TILES * STEP_BANKS + c]
-                h = h_pool.tile([P, BANK], F32)
-                nc.tensor.matmul_mx(
-                    out=h[:],
-                    lhsT=v_codes[:, tokens].bitcast(E4M3_X4),
-                    lhsT_scale=v_scales[:, tokens],
-                    rhs=codes[:].bitcast(E5M2_X4),
-                    rhs_scale=scales[:],
-                    start=True,
-                    stop=True,
-                )
-                products[s].append(h)
+            codes, scales = quantised[s // T_TILES * STEP_BANKS + c]
+            h = h_pool.tile([P, BANK], F32)
+            nc.tensor.matmul_mx(
+                out=h[:],
+                lhsT=v_codes[:, tokens].bitcast(E4M3_X4),
+                lhsT_scale=v_scales[:, tokens],
+                rhs=codes[:].bitcast(E5M2_X4),
+                rhs_scale=scales[:],
+                start=True,
+                stop=True,
+            )
+            products[(s, c)] = h
 
         def sign(s):
             even = tables[s][:, 1, :].rearrange("p (i e) -> p e i", e=2)[:, 0, :]
@@ -183,7 +193,7 @@ def tile_attention_pb_kernel(tc, Q, V, state, cos, sin, grad_out, out):
                 bank = slice(c * BANK, (c + 1) * BANK)
                 nc.vector.scalar_tensor_tensor(
                     out=term[:].rearrange("p (x n) -> p x n", x=2)[:, :, bank],
-                    in0=products[s][c][:].unsqueeze(1).to_broadcast([P, 2, BANK]),
+                    in0=products[(s, c)][:].unsqueeze(1).to_broadcast([P, 2, BANK]),
                     scalar=SCALE,
                     in1=tables[s][:, :, bank],
                     op0=MULT,
@@ -206,31 +216,21 @@ def tile_attention_pb_kernel(tc, Q, V, state, cos, sin, grad_out, out):
 
         for s in range(T_TILES):
             sign(s)
-        for b in range(STEP_BANKS):
-            flip(b)
-            quantise(b)
-        for s in range(T_TILES):
-            multiply(s)
-        flip(STEP_BANKS)
+        flip(0)
+        quantise(0)
+        flip(1)
         for s in range(STEPS):
             if s + LOAD_AHEAD < STEPS:
                 load_step(s + LOAD_AHEAD)
+            multiply(s, 0)
             if s + FLIP_AHEAD < BANKS:
                 flip(s + FLIP_AHEAD)
+            if s + 1 < BANKS:
+                quantise(s + 1)
+            multiply(s, 1)
             if T_TILES <= s + 1 < STEPS:
                 sign(s + 1)
-            if s < T_TILES:
-                rope_terms(s)
-            if s == T_TILES - 1:
-                for b in range(STEP_BANKS, 2 * STEP_BANKS):
-                    quantise(b)
-                multiply(T_TILES)
-            if s >= T_TILES:
-                if s + QUANTISE_AHEAD < BANKS:
-                    quantise(s + QUANTISE_AHEAD)
-                if s + 1 < STEPS:
-                    multiply(s + 1)
-                rope_terms(s)
+            rope_terms(s)
             if s < STEPS - 1:
                 add(nc.gpsimd, s, 0, STEP)
                 store(s, 0, STEP)

@@ -28,9 +28,10 @@ ROWS = BANK // P
 STEP_BANKS = 2
 STEP = STEP_BANKS * BANK
 STEPS = T_TILES * N // STEP
-TABLES = {0: STEP, STEP: STEP, 2 * STEP: 2 * STEP, 4 * STEP: 2 * STEP, 6 * STEP: 2 * STEP}
+TABLES = {0: STEP, STEP: 2 * STEP, 3 * STEP: 2 * STEP, 5 * STEP: 3 * STEP}
 QUANTISE_AHEAD = 1
 FLIP_AHEAD = 2
+PAIRED_STORES = 12
 LOAD_AHEAD = 10
 
 FLOPS = 2 * T * N * D
@@ -40,11 +41,11 @@ BYTES = 2 * (T * D + N * D + 2 * T * N) + 4 * T * N
 def tile_attention_pb_kernel(tc, Q, V, state, cos, sin, grad_out, out):
     nc = tc.nc
 
-    v_rows = V[0, 0, :, :].rearrange("(tt p) k -> p tt k", p=P)
+    v_rows = V[0, 0, :, :].rearrange("(p tt) k -> p (tt k)", tt=T_TILES)
     g_rows = grad_out[0, 0, :, :].rearrange("(b q r) k -> b q (r k)", q=P, r=ROWS)
-    cos_rows = cos.rearrange("(tt p) n -> tt p n", p=P)
-    sin_rows = sin.rearrange("(tt p) n -> tt p n", p=P)
-    out_rows = out[0, 0, :, :].rearrange("(tt p) n -> tt p n", p=P)
+    cos_rows = cos.rearrange("(p tt) n -> tt p n", tt=T_TILES)
+    sin_rows = sin.rearrange("(p tt) n -> tt p n", tt=T_TILES)
+    out_rows = out[0, 0, :, :].rearrange("(p tt) n -> tt p n", tt=T_TILES)
 
     with ExitStack() as ctx:
         const = ctx.enter_context(tc.tile_pool(name="const", bufs=1))
@@ -53,7 +54,7 @@ def tile_attention_pb_kernel(tc, Q, V, state, cos, sin, grad_out, out):
         grouped_pool = ctx.enter_context(tc.tile_pool(name="grouped", bufs=3))
         code_pool = ctx.enter_context(tc.tile_pool(name="code", bufs=6))
         term_pool = ctx.enter_context(tc.tile_pool(name="term", bufs=3))
-        result_pool = ctx.enter_context(tc.tile_pool(name="result", bufs=12))
+        result_pool = ctx.enter_context(tc.tile_pool(name="result", bufs=6))
         flipped_pool = ctx.enter_context(tc.psum_pool(name="flipped", bufs=4))
         h_pool = ctx.enter_context(tc.psum_pool(name="h", bufs=4))
         ctx.enter_context(tc.manual_schedule())
@@ -63,7 +64,7 @@ def tile_attention_pb_kernel(tc, Q, V, state, cos, sin, grad_out, out):
 
 
         v_sb = const.tile([P, T_TILES * D], BF16)
-        nc.sync.dma_start(out=v_sb[:].rearrange("p (tt k) -> p tt k", tt=T_TILES), in_=v_rows)
+        nc.sync.dma_start(out=v_sb[:], in_=v_rows)
         g_tiles = []
 
         def load_bank(b):
@@ -128,6 +129,7 @@ def tile_attention_pb_kernel(tc, Q, V, state, cos, sin, grad_out, out):
         grouped_tiles = {}
         quantised = {}
         terms = {}
+        pairs = {}
         results = {}
         products = {}
 
@@ -187,8 +189,11 @@ def tile_attention_pb_kernel(tc, Q, V, state, cos, sin, grad_out, out):
         def rope_terms(s):
             term = term_pool.tile([P, 2 * STEP], F32)
             terms[s] = term
-            result = result_pool.tile([P, STEP], F32)
-            results[s] = result
+            if s % (2 * T_TILES) < T_TILES:
+                result = result_pool.tile([P, 2 * STEP], F32)
+                results[s] = result[:, 0:STEP]
+                results[s + T_TILES] = result[:, STEP:]
+                pairs[s] = result
             for c in range(STEP_BANKS):
                 bank = slice(c * BANK, (c + 1) * BANK)
                 nc.vector.scalar_tensor_tensor(
@@ -214,6 +219,12 @@ def tile_attention_pb_kernel(tc, Q, V, state, cos, sin, grad_out, out):
                 in_=results[s][:, first : first + width],
             )
 
+        def store_pair(s):
+            columns = s // T_TILES * STEP
+            nc.sync.dma_start(
+                out=out_rows[s % T_TILES, :, columns : columns + 2 * STEP], in_=pairs[s][:]
+            )
+
         for s in range(T_TILES):
             sign(s)
         flip(0)
@@ -233,7 +244,10 @@ def tile_attention_pb_kernel(tc, Q, V, state, cos, sin, grad_out, out):
             rope_terms(s)
             if s < STEPS - 1:
                 add(nc.gpsimd, s, 0, STEP)
-                store(s, 0, STEP)
+                if s >= PAIRED_STORES:
+                    store(s, 0, STEP)
+                elif s - T_TILES in pairs:
+                    store_pair(s - T_TILES)
             else:
                 for c in range(STEP_BANKS):
                     add(nc.vector, s, c * BANK, BANK)

@@ -32,6 +32,7 @@ TABLES = {0: STEP, STEP: 2 * STEP, 3 * STEP: 2 * STEP, 5 * STEP: 3 * STEP}
 QUANTISE_AHEAD = 1
 FLIP_AHEAD = 2
 PAIRED_STORES = 12
+SINGLE_BANKS = 8
 LOAD_AHEAD = 10
 
 FLOPS = 2 * T * N * D
@@ -43,15 +44,16 @@ def tile_attention_pb_kernel(tc, Q, V, state, cos, sin, grad_out, out):
 
     v_rows = V[0, 0, :, :].rearrange("(p tt) k -> p (tt k)", tt=T_TILES)
     g_rows = grad_out[0, 0, :, :].rearrange("(b q r) k -> b q (r k)", q=P, r=ROWS)
+    g_pair_rows = grad_out[0, 0, :, :].rearrange("(b q r) k -> b q (r k)", q=P, r=2 * ROWS)
     cos_rows = cos.rearrange("(p tt) n -> tt p n", tt=T_TILES)
     sin_rows = sin.rearrange("(p tt) n -> tt p n", tt=T_TILES)
     out_rows = out[0, 0, :, :].rearrange("(p tt) n -> tt p n", tt=T_TILES)
 
     with ExitStack() as ctx:
         const = ctx.enter_context(tc.tile_pool(name="const", bufs=1))
-        g_pool = ctx.enter_context(tc.tile_pool(name="g", bufs=BANKS))
+        g_pool = ctx.enter_context(tc.tile_pool(name="g", bufs=1))
         table_pool = ctx.enter_context(tc.tile_pool(name="table", bufs=1))
-        grouped_pool = ctx.enter_context(tc.tile_pool(name="grouped", bufs=3))
+        grouped_pool = ctx.enter_context(tc.tile_pool(name="grouped", bufs=2))
         code_pool = ctx.enter_context(tc.tile_pool(name="code", bufs=6))
         term_pool = ctx.enter_context(tc.tile_pool(name="term", bufs=3))
         result_pool = ctx.enter_context(tc.tile_pool(name="result", bufs=6))
@@ -68,9 +70,15 @@ def tile_attention_pb_kernel(tc, Q, V, state, cos, sin, grad_out, out):
         g_tiles = []
 
         def load_bank(b):
-            g_sb = g_pool.tile([P, ROWS * D], BF16)
-            nc.sync.dma_start(out=g_sb[:], in_=g_rows[b])
-            g_tiles.append(g_sb)
+            if b < SINGLE_BANKS:
+                g_sb = g_pool.tile([P, ROWS * D], BF16, name="g_%d" % b)
+                nc.sync.dma_start(out=g_sb[:], in_=g_rows[b])
+                g_tiles.append(g_sb[:])
+            elif b % 2 == 0:
+                g_sb = g_pool.tile([P, 2 * ROWS * D], BF16, name="g_%d" % b)
+                nc.sync.dma_start(out=g_sb[:], in_=g_pair_rows[b // 2])
+                g_tiles.append(g_sb[:, 0 : ROWS * D])
+                g_tiles.append(g_sb[:, ROWS * D :])
 
         tables = {}
         table_tiles = {}
@@ -134,10 +142,16 @@ def tile_attention_pb_kernel(tc, Q, V, state, cos, sin, grad_out, out):
         products = {}
 
         def flip(b):
-            g_words = g_tiles[b][:].bitcast(F32)
-            grouped = grouped_pool.tile([P, BANK * PACK], BF16, align_bytes=64)
-            grouped_tiles[b] = grouped
-            grouped_words = grouped[:].bitcast(F32).rearrange("p (q m w) -> p m q w", m=2, w=4)
+            g_words = g_tiles[b].bitcast(F32)
+            half = b % 2
+            if half == 0:
+                grouped = grouped_pool.tile([P, 2 * BANK * PACK], BF16, align_bytes=64)
+                grouped_tiles[b // 2] = grouped
+            words = grouped_tiles[b // 2][:].bitcast(F32)
+            if b < SINGLE_BANKS:
+                places = words.rearrange("p (h q m w) -> p h m q w", h=2, m=2, w=4)[:, half]
+            else:
+                places = words.rearrange("p (q h m w) -> p h m q w", h=2, m=2, w=4)[:, half]
             for m in range(2):
                 flipped = flipped_pool.tile([P, BANK], F32, tag="flipped")
                 for e in range(2):
@@ -150,7 +164,7 @@ def tile_attention_pb_kernel(tc, Q, V, state, cos, sin, grad_out, out):
                             identity[:],
                         )
                 nc.scalar.copy(
-                    out=grouped_words[:, m, :, :],
+                    out=places[:, m, :, :],
                     in_=flipped[:].rearrange("p (w q) -> p q w", w=4),
                 )
 
@@ -158,7 +172,7 @@ def tile_attention_pb_kernel(tc, Q, V, state, cos, sin, grad_out, out):
             codes = code_pool.tile([P, BANK], U32, align_bytes=64)
             scales = code_pool.tile([P, BANK], U8, align_bytes=64)
             nc.vector.quantize_mx(
-                out=codes[:].bitcast(E5M2_X4), scales=scales[:], in_=grouped_tiles[b][:]
+                out=codes[:].bitcast(E5M2_X4), scales=scales[:], in_=grouped_tiles[b // 2][:, b % 2 * BANK * PACK : (b % 2 + 1) * BANK * PACK]
             )
             quantised[b] = (codes, scales)
 
@@ -230,12 +244,16 @@ def tile_attention_pb_kernel(tc, Q, V, state, cos, sin, grad_out, out):
         flip(0)
         quantise(0)
         flip(1)
+        flipped_banks = [2]
         for s in range(STEPS):
             if s + LOAD_AHEAD < STEPS:
                 load_step(s + LOAD_AHEAD)
             multiply(s, 0)
-            if s + FLIP_AHEAD < BANKS:
-                flip(s + FLIP_AHEAD)
+            due = [b for b in (s + FLIP_AHEAD, s + FLIP_AHEAD + 1) if flipped_banks[0] <= b < BANKS]
+            for b in due:
+                if b == s + FLIP_AHEAD or (b >= SINGLE_BANKS and b % 2 == 1):
+                    flip(b)
+                    flipped_banks[0] = b + 1
             if s + 1 < BANKS:
                 quantise(s + 1)
             multiply(s, 1)

@@ -211,7 +211,7 @@ def tile_attention_pb_kernel(tc, Q, V, state, cos, sin, grad_out, out):
             for c in range(STEP_BANKS):
                 bank = slice(c * BANK, (c + 1) * BANK)
                 nc.vector.scalar_tensor_tensor(
-                    out=term[:].rearrange("p (x n) -> p x n", x=2)[:, :, bank],
+                    out=term[:].rearrange("p (c x n) -> p c x n", c=STEP_BANKS, x=2)[:, c],
                     in0=products[(s, c)][:].unsqueeze(1).to_broadcast([P, 2, BANK]),
                     scalar=SCALE,
                     in1=tables[s][:, :, bank],
@@ -219,12 +219,15 @@ def tile_attention_pb_kernel(tc, Q, V, state, cos, sin, grad_out, out):
                     op1=MULT,
                 )
 
-        def add(engine, s, first, width):
-            own, other, out = (
-                t[:, c : c + width].rearrange("p (i e) -> p i e", e=2)
-                for t, c in ((terms[s], first), (terms[s], STEP + first), (results[s], first))
+        def add(engine, s, c, count):
+            term = terms[s][:].rearrange("p (c x i e) -> p c x i e", c=STEP_BANKS, x=2, e=2)
+            out = results[s].rearrange("p (c i e) -> p c i e", c=STEP_BANKS, e=2)
+            engine.tensor_tensor(
+                out=out[:, c : c + count],
+                in0=term[:, c : c + count, 0],
+                in1=term[:, c : c + count, 1, :, ::-1],
+                op=ADD,
             )
-            engine.tensor_tensor(out=out, in0=own, in1=other[:, :, ::-1], op=ADD)
 
         def store(s, first, width):
             columns = s // T_TILES * STEP + first
@@ -261,12 +264,12 @@ def tile_attention_pb_kernel(tc, Q, V, state, cos, sin, grad_out, out):
                 sign(s + 1)
             rope_terms(s)
             if s < STEPS - 1:
-                add(nc.gpsimd, s, 0, STEP)
+                add(nc.gpsimd, s, 0, STEP_BANKS)
                 if s >= PAIRED_STORES:
                     store(s, 0, STEP)
                 elif s - T_TILES in pairs:
                     store_pair(s - T_TILES)
             else:
                 for c in range(STEP_BANKS):
-                    add(nc.vector, s, c * BANK, BANK)
+                    add(nc.vector, s, c, 1)
                     store(s, c * BANK, BANK)

@@ -31,9 +31,10 @@ STEPS = T_TILES * N // STEP
 TABLES = {0: STEP, STEP: 2 * STEP, 3 * STEP: 2 * STEP, 5 * STEP: 3 * STEP}
 QUANTISE_AHEAD = 1
 FLIP_AHEAD = 2
-PAIRED_STORES = 12
+STORES = {0: 5, 5: 1, 6: 1, 7: 1}
 SINGLE_BANKS = 8
-LOAD_AHEAD = 10
+G_SLOTS = 4
+LOAD_AHEAD = 7
 
 FLOPS = 2 * T * N * D
 BYTES = 2 * (T * D + N * D + 2 * T * N) + 4 * T * N
@@ -56,7 +57,7 @@ def tile_attention_pb_kernel(tc, Q, V, state, cos, sin, grad_out, out):
         grouped_pool = ctx.enter_context(tc.tile_pool(name="grouped", bufs=2))
         code_pool = ctx.enter_context(tc.tile_pool(name="code", bufs=6))
         term_pool = ctx.enter_context(tc.tile_pool(name="term", bufs=3))
-        result_pool = ctx.enter_context(tc.tile_pool(name="result", bufs=6))
+        result_pool = ctx.enter_context(tc.tile_pool(name="result", bufs=1))
         flipped_pool = ctx.enter_context(tc.psum_pool(name="flipped", bufs=4))
         h_pool = ctx.enter_context(tc.psum_pool(name="h", bufs=4))
         ctx.enter_context(tc.manual_schedule())
@@ -70,15 +71,14 @@ def tile_attention_pb_kernel(tc, Q, V, state, cos, sin, grad_out, out):
         g_tiles = []
 
         def load_bank(b):
-            if b < SINGLE_BANKS:
-                g_sb = g_pool.tile([P, ROWS * D], BF16, name="g_%d" % b)
-                nc.sync.dma_start(out=g_sb[:], in_=g_rows[b])
-                g_tiles.append(g_sb[:])
-            elif b % 2 == 0:
-                g_sb = g_pool.tile([P, 2 * ROWS * D], BF16, name="g_%d" % b)
-                nc.sync.dma_start(out=g_sb[:], in_=g_pair_rows[b // 2])
+            if b % 2 == 0:
+                g_sb = g_pool.tile([P, 2 * ROWS * D], BF16, name="g_%d" % (b // 2 % G_SLOTS))
                 g_tiles.append(g_sb[:, 0 : ROWS * D])
                 g_tiles.append(g_sb[:, ROWS * D :])
+                if b >= SINGLE_BANKS:
+                    nc.sync.dma_start(out=g_sb[:], in_=g_pair_rows[b // 2])
+            if b < SINGLE_BANKS:
+                nc.sync.dma_start(out=g_tiles[b], in_=g_rows[b])
 
         tables = {}
         table_tiles = {}
@@ -113,7 +113,7 @@ def tile_attention_pb_kernel(tc, Q, V, state, cos, sin, grad_out, out):
         load_table(1, 1)
         load_bank(3)
         load_table(1, 0)
-        for s in range(T_TILES, LOAD_AHEAD):
+        for s in range(T_TILES, LOAD_AHEAD - 1):
             load_step(s)
 
         v_words = v_sb[:].bitcast(F32)
@@ -137,7 +137,7 @@ def tile_attention_pb_kernel(tc, Q, V, state, cos, sin, grad_out, out):
         grouped_tiles = {}
         quantised = {}
         terms = {}
-        pairs = {}
+        wholes = {}
         results = {}
         products = {}
 
@@ -203,11 +203,12 @@ def tile_attention_pb_kernel(tc, Q, V, state, cos, sin, grad_out, out):
         def rope_terms(s):
             term = term_pool.tile([P, 2 * STEP], F32)
             terms[s] = term
-            if s % (2 * T_TILES) < T_TILES:
-                result = result_pool.tile([P, 2 * STEP], F32)
-                results[s] = result[:, 0:STEP]
-                results[s + T_TILES] = result[:, STEP:]
-                pairs[s] = result
+            block = s // T_TILES
+            if block in STORES:
+                result = result_pool.tile([P, STORES[block] * STEP], F32, name="result_%d" % s)
+                for i in range(STORES[block]):
+                    results[s + T_TILES * i] = result[:, i * STEP : (i + 1) * STEP]
+                wholes[s] = result
             for c in range(STEP_BANKS):
                 bank = slice(c * BANK, (c + 1) * BANK)
                 nc.vector.scalar_tensor_tensor(
@@ -233,13 +234,7 @@ def tile_attention_pb_kernel(tc, Q, V, state, cos, sin, grad_out, out):
             columns = s // T_TILES * STEP + first
             nc.sync.dma_start(
                 out=out_rows[s % T_TILES, :, columns : columns + width],
-                in_=results[s][:, first : first + width],
-            )
-
-        def store_pair(s):
-            columns = s // T_TILES * STEP
-            nc.sync.dma_start(
-                out=out_rows[s % T_TILES, :, columns : columns + 2 * STEP], in_=pairs[s][:]
+                in_=wholes[s][:, first : first + width],
             )
 
         for s in range(T_TILES):
@@ -247,10 +242,9 @@ def tile_attention_pb_kernel(tc, Q, V, state, cos, sin, grad_out, out):
         flip(0)
         quantise(0)
         flip(1)
+        load_step(LOAD_AHEAD - 1)
         flipped_banks = [2]
         for s in range(STEPS):
-            if s + LOAD_AHEAD < STEPS:
-                load_step(s + LOAD_AHEAD)
             multiply(s, 0)
             due = [b for b in (s + FLIP_AHEAD, s + FLIP_AHEAD + 1) if flipped_banks[0] <= b < BANKS]
             for b in due:
@@ -263,13 +257,14 @@ def tile_attention_pb_kernel(tc, Q, V, state, cos, sin, grad_out, out):
             if T_TILES <= s + 1 < STEPS:
                 sign(s + 1)
             rope_terms(s)
-            if s < STEPS - 1:
+            if s + LOAD_AHEAD < STEPS:
+                load_step(s + LOAD_AHEAD)
+            if s < STEPS - 2:
                 add(nc.gpsimd, s, 0, STEP_BANKS)
-                if s >= PAIRED_STORES:
-                    store(s, 0, STEP)
-                elif s - T_TILES in pairs:
-                    store_pair(s - T_TILES)
+                for first, blocks in STORES.items():
+                    if s // T_TILES == first + blocks - 1:
+                        store(first * T_TILES + s % T_TILES, 0, blocks * STEP)
             else:
                 for c in range(STEP_BANKS):
-                    add(nc.vector, s, c, 1)
+                    add(nc.vector if s == STEPS - 1 else nc.gpsimd, s, c, 1)
                     store(s, c * BANK, BANK)

from contextlib import ExitStack

import concourse.mybir as mybir
from concourse.masks import make_identity

F32 = mybir.dt.float32
BF16 = mybir.dt.bfloat16
U32 = mybir.dt.uint32
U8 = mybir.dt.uint8
E4M3_X4 = mybir.dt.float8_e4m3fn_x4
E5M2_X4 = mybir.dt.float8_e5m2_x4
COPY = mybir.ActivationFunctionType.Copy
MULT = mybir.AluOpType.mult
ADD = mybir.AluOpType.add

P = 128
T = 256
D = 512
N = 8192
SCALE = N**-0.5

PACK = 4
WORDS = D // 2
T_TILES = T // P
BANK = 512
BANKS = N // BANK
ROWS = BANK // P
STEP_BANKS = 2
STEP = STEP_BANKS * BANK
STEPS = T_TILES * N // STEP
TABLES = {0: STEP, STEP: 2 * STEP, 3 * STEP: 2 * STEP, 5 * STEP: 3 * STEP}
QUANTISE_AHEAD = 1
FLIP_AHEAD = 2
STORES = {0: 5, 5: 1, 6: 1, 7: 1}
SINGLE_BANKS = 8
G_SLOTS = 4
LOAD_AHEAD = 7

FLOPS = 2 * T * N * D
BYTES = 2 * (T * D + N * D + 2 * T * N) + 4 * T * N


def tile_attention_pb_kernel(tc, Q, V, state, cos, sin, grad_out, out):
    nc = tc.nc

    v_rows = V[0, 0, :, :].rearrange("(p tt) k -> p (tt k)", tt=T_TILES)
    g_rows = grad_out[0, 0, :, :].rearrange("(b q r) k -> b q (r k)", q=P, r=ROWS)
    g_pair_rows = grad_out[0, 0, :, :].rearrange("(b q r) k -> b q (r k)", q=P, r=2 * ROWS)
    cos_rows = cos.rearrange("(p tt) n -> tt p n", tt=T_TILES)
    sin_rows = sin.rearrange("(p tt) n -> tt p n", tt=T_TILES)
    out_rows = out[0, 0, :, :].rearrange("(p tt) n -> tt p n", tt=T_TILES)

    with ExitStack() as ctx:
        const = ctx.enter_context(tc.tile_pool(name="const", bufs=1))
        g_pool = ctx.enter_context(tc.tile_pool(name="g", bufs=1))
        table_pool = ctx.enter_context(tc.tile_pool(name="table", bufs=1))
        grouped_pool = ctx.enter_context(tc.tile_pool(name="grouped", bufs=2))
        code_pool = ctx.enter_context(tc.tile_pool(name="code", bufs=6))
        term_pool = ctx.enter_context(tc.tile_pool(name="term", bufs=3))
        result_pool = ctx.enter_context(tc.tile_pool(name="result", bufs=1))
        flipped_pool = ctx.enter_context(tc.psum_pool(name="flipped", bufs=4))
        h_pool = ctx.enter_context(tc.psum_pool(name="h", bufs=4))
        ctx.enter_context(tc.manual_schedule())

        identity = const.tile([P, P], F32)
        make_identity(nc, identity[:])


        v_sb = const.tile([P, T_TILES * D], BF16)
        nc.sync.dma_start(out=v_sb[:], in_=v_rows)
        g_tiles = []

        def load_bank(b):
            if b % 2 == 0:
                g_sb = g_pool.tile([P, 2 * ROWS * D], BF16, name="g_%d" % (b // 2 % G_SLOTS))
                g_tiles.append(g_sb[:, 0 : ROWS * D])
                g_tiles.append(g_sb[:, ROWS * D :])
                if b >= SINGLE_BANKS:
                    nc.sync.dma_start(out=g_sb[:], in_=g_pair_rows[b // 2])
            if b < SINGLE_BANKS:
                nc.sync.dma_start(out=g_tiles[b], in_=g_rows[b])

        tables = {}
        table_tiles = {}

        def load_table(s, x):
            tt = s % T_TILES
            first = s // T_TILES * STEP
            if first in TABLES:
                width = TABLES[first]
                if s not in table_tiles:
                    table = table_pool.tile([P, 2 * width], BF16, name="table_%d" % s)
                    table_tiles[s] = table
                    planes = table[:].rearrange("p (x n) -> p x n", x=2)
                    for c in range(width // STEP):
                        tables[s + T_TILES * c] = planes[:, :, c * STEP : (c + 1) * STEP]
                nc.sync.dma_start(
                    out=table_tiles[s][:, x * width : (x + 1) * width],
                    in_=(cos_rows, sin_rows)[x][tt, :, first : first + width],
                )

        def load_step(s):
            load_table(s, 1)
            load_table(s, 0)
            if s + FLIP_AHEAD < BANKS:
                load_bank(s + FLIP_AHEAD)

        load_bank(0)
        load_table(0, 1)
        load_bank(1)
        load_table(0, 0)
        load_bank(2)
        load_table(1, 1)
        load_bank(3)
        load_table(1, 0)
        for s in range(T_TILES, LOAD_AHEAD - 1):
            load_step(s)

        v_words = v_sb[:].bitcast(F32)
        v_flipped = flipped_pool.tile([P, BANK], F32, tag="flipped")
        for u in range(2):
            for tt in range(T_TILES):
                nc.tensor.transpose(
                    v_flipped[:, (u * T_TILES + tt) * P : (u * T_TILES + tt + 1) * P],
                    v_words[:, tt * WORDS + u * P : tt * WORDS + (u + 1) * P],
                    identity[:],
                )
        v_grouped = const.tile([P, T * PACK], BF16, align_bytes=64)
        nc.vector.tensor_copy(
            out=v_grouped[:].bitcast(F32).rearrange("p (t u) -> p t u", u=2),
            in_=v_flipped[:].rearrange("p (u t) -> p t u", u=2),
        )
        v_codes = const.tile([P, T], U32, align_bytes=64)
        v_scales = const.tile([P, T], U8, align_bytes=64)
        nc.vector.quantize_mx(out=v_codes[:].bitcast(E4M3_X4), scales=v_scales[:], in_=v_grouped[:])

        grouped_tiles = {}
        quantised = {}
        terms = {}
        wholes = {}
        results = {}
        products = {}

        def flip(b):
            g_words = g_tiles[b].bitcast(F32)
            half = b % 2
            if half == 0:
                grouped = grouped_pool.tile([P, 2 * BANK * PACK], BF16, align_bytes=64)
                grouped_tiles[b // 2] = grouped
            words = grouped_tiles[b // 2][:].bitcast(F32)
            if b < SINGLE_BANKS:
                places = words.rearrange("p (h q m w) -> p h m q w", h=2, m=2, w=4)[:, half]
            else:
                places = words.rearrange("p (q h m w) -> p h m q w", h=2, m=2, w=4)[:, half]
            for m in range(2):
                flipped = flipped_pool.tile([P, BANK], F32, tag="flipped")
                for e in range(2):
                    for u in range(2):
                        r = 2 * m + e
                        w = 2 * e + u
                        nc.tensor.transpose(
                            flipped[:, w * P : (w + 1) * P],
                            g_words[:, r * WORDS + u * P : r * WORDS + (u + 1) * P],
                            identity[:],
                        )
                nc.scalar.copy(
                    out=places[:, m, :, :],
                    in_=flipped[:].rearrange("p (w q) -> p q w", w=4),
                )

        def quantise(b):
            codes = code_pool.tile([P, BANK], U32, align_bytes=64)
            scales = code_pool.tile([P, BANK], U8, align_bytes=64)
            nc.vector.quantize_mx(
                out=codes[:].bitcast(E5M2_X4), scales=scales[:], in_=grouped_tiles[b // 2][:, b % 2 * BANK * PACK : (b % 2 + 1) * BANK * PACK]
            )
            quantised[b] = (codes, scales)

        def multiply(s, c):
            tokens = slice(s % T_TILES * P, (s % T_TILES + 1) * P)
            codes, scales = quantised[s // T_TILES * STEP_BANKS + c]
            h = h_pool.tile([P, BANK], F32)
            nc.tensor.matmul_mx(
                out=h[:],
                lhsT=v_codes[:, tokens].bitcast(E4M3_X4),
                lhsT_scale=v_scales[:, tokens],
                rhs=codes[:].bitcast(E5M2_X4),
                rhs_scale=scales[:],
                start=True,
                stop=True,
            )
            products[(s, c)] = h

        def sign(s):
            even = tables[s][:, 1, :].rearrange("p (i e) -> p e i", e=2)[:, 0, :]
            if s < T_TILES:
                nc.gpsimd.tensor_scalar(
                    out=even, in0=even, scalar1=-1.0, scalar2=0.0, op0=MULT, op1=ADD
                )
            else:
                nc.scalar.activation(out=even, in_=even, func=COPY, scale=-1.0)

        def rope_terms(s):
            term = term_pool.tile([P, 2 * STEP], F32)
            terms[s] = term
            block = s // T_TILES
            if block in STORES:
                result = result_pool.tile([P, STORES[block] * STEP], F32, name="result_%d" % s)
                for i in range(STORES[block]):
                    results[s + T_TILES * i] = result[:, i * STEP : (i + 1) * STEP]
                wholes[s] = result
            for c in range(STEP_BANKS):
                bank = slice(c * BANK, (c + 1) * BANK)
                nc.vector.scalar_tensor_tensor(
                    out=term[:].rearrange("p (c x n) -> p c x n", c=STEP_BANKS, x=2)[:, c],
                    in0=products[(s, c)][:].unsqueeze(1).to_broadcast([P, 2, BANK]),
                    scalar=SCALE,
                    in1=tables[s][:, :, bank],
                    op0=MULT,
                    op1=MULT,
                )

        def add(engine, s, c, count):
            term = terms[s][:].rearrange("p (c x i e) -> p c x i e", c=STEP_BANKS, x=2, e=2)
            out = results[s].rearrange("p (c i e) -> p c i e", c=STEP_BANKS, e=2)
            engine.tensor_tensor(
                out=out[:, c : c + count],
                in0=term[:, c : c + count, 0],
                in1=term[:, c : c + count, 1, :, ::-1],
                op=ADD,
            )

        def store(s, first, width):
            columns = s // T_TILES * STEP + first
            nc.sync.dma_start(
                out=out_rows[s % T_TILES, :, columns : columns + width],
                in_=wholes[s][:, first : first + width],
            )

        for s in range(T_TILES):
            sign(s)
        flip(0)
        quantise(0)
        flip(1)
        load_step(LOAD_AHEAD - 1)
        flipped_banks = [2]
        for s in range(STEPS):
            multiply(s, 0)
            due = [b for b in (s + FLIP_AHEAD, s + FLIP_AHEAD + 1) if flipped_banks[0] <= b < BANKS]
            for b in due:
                if b == s + FLIP_AHEAD or (b >= SINGLE_BANKS and b % 2 == 1):
                    flip(b)
                    flipped_banks[0] = b + 1
            if s + 1 < BANKS:
                quantise(s + 1)
            multiply(s, 1)
            if T_TILES <= s + 1 < STEPS:
                sign(s + 1)
            rope_terms(s)
            if s + LOAD_AHEAD < STEPS:
                load_step(s + LOAD_AHEAD)
            if s < STEPS - 2:
                add(nc.gpsimd, s, 0, STEP_BANKS)
                for first, blocks in STORES.items():
                    if s // T_TILES == first + blocks - 1:
                        store(first * T_TILES + s % T_TILES, 0, blocks * STEP)
            else:
                for c in range(STEP_BANKS):
                    add(nc.vector if s == STEPS - 1 else nc.gpsimd, s, c, 1)
                    store(s, c * BANK, BANK)
